import numpy as np
import ml_dtypes

BF16 = ml_dtypes.bfloat16


def bf(x):
    return np.asarray(x, np.float32).astype(BF16)


def f32(x):
    return np.asarray(x, np.float32)


def f64(x):
    return np.asarray(x).astype(np.float64)


def striped(idx):
    return np.tile(idx.reshape(-1, 16).T, (8, 1))


C, S, N, K, G = 128, 1024, 512, 4, 128


def setup_inputs():
    return {"table": bf(np.random.standard_normal((C, S))), "w": bf(np.random.standard_normal((C, K * G)) / np.sqrt(C * K)), "ew": f32(np.random.standard_normal((K, N))), "b": f32(0.2 * np.random.standard_normal((G, 1))), "offs": striped(np.random.permutation(S)[:N])}


def reference(table, w, ew, b, offs):
    idx = offs[:16].T.reshape(-1)
    p = (f64(w).T @ f64(table)[:, idx]).reshape(K, G, N)
    y = (p * f64(ew)[:, None, :]).sum(axis=0)
    return np.maximum(y + f64(b), 0.0)

@@ -1,0 +1,62 @@
+import concourse.mybir as mybir
+
+C = 128
+S = 1024
+N = 512
+K = 4
+G = 128
+
+FLOPS = 2 * C * K * G * N
+
+BF16 = mybir.dt.bfloat16
+F32 = mybir.dt.float32
+U16 = mybir.dt.uint16
+MULT = mybir.AluOpType.mult
+ADD = mybir.AluOpType.add
+RELU = mybir.ActivationFunctionType.Relu
+
+
+def tile_sgcn_kernel(tc, table, w, ew, b, offs, out):
+    nc = tc.nc
+    with (
+        tc.tile_pool(name="held", bufs=1) as held,
+        tc.tile_pool(name="work", bufs=2) as work,
+        tc.psum_pool(name="psum", bufs=1) as psum,
+    ):
+        offsets = held.tile([128, N // 16], U16, name="offsets")
+        nc.sync.dma_start(offsets[:], offs)
+        nodes = held.tile([C, S], BF16, name="nodes")
+        nc.sync.dma_start(nodes[:], table)
+        kernels = held.tile([C, K * G], BF16, name="kernels")
+        nc.scalar.dma_start(kernels[:], w)
+
+        edge_weights = []
+        for k in range(K):
+            row = held.tile([G, N], F32, name=f"edge_weights{k}")
+            nc.scalar.dma_start(row[:], ew[k, :].partition_broadcast(G))
+            edge_weights.append(row)
+        bias = held.tile([G, 1], F32, name="bias")
+        nc.sync.dma_start(bias[:], b)
+
+        projected = []
+        for k in range(K):
+            bank = psum.tile([G, N], F32, name=f"projected{k}")
+            nc.tensor.matmul(
+                bank[:],
+                kernels[:, k * G : (k + 1) * G],
+                nodes[:].indirect(offsets[:]),
+                start=True,
+                stop=True,
+            )
+            projected.append(bank)
+
+        mixed = held.tile([G, N], F32, name="mixed")
+        nc.vector.tensor_tensor(mixed[:], projected[0][:], edge_weights[0][:], MULT)
+        for k in range(1, K):
+            weighted = work.tile([G, N], F32, name="weighted")
+            nc.vector.tensor_tensor(weighted[:], projected[k][:], edge_weights[k][:], MULT)
+            nc.vector.tensor_tensor(mixed[:], mixed[:], weighted[:], ADD)
+
+        result = held.tile([G, N], F32, name="result")
+        nc.scalar.activation(result[:], mixed[:], RELU, bias=bias[:, 0:1])
+        nc.sync.dma_start(out, result[:])

@@ -8,6 +8,8 @@ G = 128
 
 FLOPS = 2 * C * K * G * N
 
+WARM_UP = 5
+
 BF16 = mybir.dt.bfloat16
 F32 = mybir.dt.float32
 U16 = mybir.dt.uint16
@@ -37,6 +39,12 @@ def tile_sgcn_kernel(tc, table, w, ew, b, offs, out):
             edge_weights.append(row)
         bias = held.tile([G, 1], F32, name="bias")
         nc.sync.dma_start(bias[:], b)
+
+        zeros = held.tile([C, N], BF16, name="zeros")
+        nc.gpsimd.memset(zeros[:], 0.0)
+        unread = psum.tile([G, N], F32, name="unread")
+        for repeat in range(WARM_UP):
+            nc.tensor.matmul(unread[:], zeros[:, 0:G], zeros[:], start=True, stop=True)
 
         projected = []
         for k in range(K):

@@ -8,21 +8,18 @@ G = 128
 
 FLOPS = 2 * C * K * G * N
 
-WARM_UP = 5
-
 BF16 = mybir.dt.bfloat16
 F32 = mybir.dt.float32
 U16 = mybir.dt.uint16
 MULT = mybir.AluOpType.mult
 ADD = mybir.AluOpType.add
-RELU = mybir.ActivationFunctionType.Relu
+MAX = mybir.AluOpType.max
 
 
 def tile_sgcn_kernel(tc, table, w, ew, b, offs, out):
     nc = tc.nc
     with (
         tc.tile_pool(name="held", bufs=1) as held,
-        tc.tile_pool(name="work", bufs=2) as work,
         tc.psum_pool(name="psum", bufs=1) as psum,
     ):
         offsets = held.tile([128, N // 16], U16, name="offsets")
@@ -40,12 +37,6 @@ def tile_sgcn_kernel(tc, table, w, ew, b, offs, out):
         bias = held.tile([G, 1], F32, name="bias")
         nc.sync.dma_start(bias[:], b)
 
-        zeros = held.tile([C, N], BF16, name="zeros")
-        nc.gpsimd.memset(zeros[:], 0.0)
-        unread = psum.tile([G, N], F32, name="unread")
-        for repeat in range(WARM_UP):
-            nc.tensor.matmul(unread[:], zeros[:, 0:G], zeros[:], start=True, stop=True)
-
         projected = []
         for k in range(K):
             bank = psum.tile([G, N], F32, name=f"projected{k}")
@@ -58,13 +49,16 @@ def tile_sgcn_kernel(tc, table, w, ew, b, offs, out):
             )
             projected.append(bank)
 
-        mixed = held.tile([G, N], F32, name="mixed")
-        nc.vector.tensor_tensor(mixed[:], projected[0][:], edge_weights[0][:], MULT)
-        for k in range(1, K):
-            weighted = work.tile([G, N], F32, name="weighted")
-            nc.vector.tensor_tensor(weighted[:], projected[k][:], edge_weights[k][:], MULT)
-            nc.vector.tensor_tensor(mixed[:], mixed[:], weighted[:], ADD)
+        weighted = []
+        for k in range(K + 1):
+            if k < K:
+                product = held.tile([G, N], F32, name=f"weighted{k}")
+                nc.vector.tensor_tensor(product[:], projected[k][:], edge_weights[k][:], MULT)
+                weighted.append(product)
+            if k >= 2:
+                nc.vector.tensor_tensor(weighted[0][:], weighted[0][:], weighted[k - 1][:], ADD)
+        mixed = weighted[0]
 
         result = held.tile([G, N], F32, name="result")
-        nc.scalar.activation(result[:], mixed[:], RELU, bias=bias[:, 0:1])
+        nc.vector.tensor_scalar(result[:], mixed[:], bias[:, 0:1], 0.0, op0=ADD, op1=MAX)
         nc.sync.dma_start(out, result[:])

@@ -8,6 +8,8 @@ G = 128
 
 FLOPS = 2 * C * K * G * N
 
+WARM_UP = 4
+
 BF16 = mybir.dt.bfloat16
 F32 = mybir.dt.float32
 U16 = mybir.dt.uint16
@@ -36,6 +38,12 @@ def tile_sgcn_kernel(tc, table, w, ew, b, offs, out):
             edge_weights.append(row)
         bias = held.tile([G, 1], F32, name="bias")
         nc.sync.dma_start(bias[:], b)
+
+        zeros = held.tile([C, N], BF16, name="zeros")
+        nc.vector.memset(zeros[:], 0.0)
+        unread = psum.tile([G, N], F32, name="unread")
+        for repeat in range(WARM_UP):
+            nc.tensor.matmul(unread[:], zeros[:, 0:G], zeros[:], start=True, stop=True)
 
         projected = []
         for k in range(K):

@@ -5,10 +5,10 @@ S = 1024
 N = 512
 K = 4
 G = 128
+HALVES = 2
+H = N // HALVES
 
 FLOPS = 2 * C * K * G * N
-
-WARM_UP = 4
 
 BF16 = mybir.dt.bfloat16
 F32 = mybir.dt.float32
@@ -39,34 +39,43 @@ def tile_sgcn_kernel(tc, table, w, ew, b, offs, out):
         bias = held.tile([G, 1], F32, name="bias")
         nc.sync.dma_start(bias[:], b)
 
-        zeros = held.tile([C, N], BF16, name="zeros")
-        nc.vector.memset(zeros[:], 0.0)
-        unread = psum.tile([G, N], F32, name="unread")
-        for repeat in range(WARM_UP):
-            nc.tensor.matmul(unread[:], zeros[:, 0:G], zeros[:], start=True, stop=True)
+        projected = [
+            [psum.tile([G, H], F32, name=f"projected{k}_{h}") for h in range(HALVES)]
+            for k in range(K)
+        ]
 
-        projected = []
         for k in range(K):
-            bank = psum.tile([G, N], F32, name=f"projected{k}")
-            nc.tensor.matmul(
-                bank[:],
-                kernels[:, k * G : (k + 1) * G],
-                nodes[:].indirect(offsets[:]),
-                start=True,
-                stop=True,
-            )
-            projected.append(bank)
+            for h in range(HALVES):
+                nc.tensor.matmul(
+                    projected[k][h][:],
+                    kernels[:, k * G : (k + 1) * G],
+                    nodes[:].indirect(offsets[:, h * (H // 16) : (h + 1) * (H // 16)]),
+                    start=True,
+                    stop=True,
+                )
 
-        weighted = []
+        weighted = [held.tile([G, N], F32, name=f"weighted{k}") for k in range(K)]
+        mixed = weighted[0]
+        pieces = [slice(h * H, (h + 1) * H) for h in range(HALVES)]
         for k in range(K + 1):
             if k < K:
-                product = held.tile([G, N], F32, name=f"weighted{k}")
-                nc.vector.tensor_tensor(product[:], projected[k][:], edge_weights[k][:], MULT)
-                weighted.append(product)
+                for h in range(HALVES):
+                    nc.vector.tensor_tensor(
+                        weighted[k][:, pieces[h]],
+                        projected[k][h][:],
+                        edge_weights[k][:, pieces[h]],
+                        MULT,
+                    )
             if k >= 2:
-                nc.vector.tensor_tensor(weighted[0][:], weighted[0][:], weighted[k - 1][:], ADD)
-        mixed = weighted[0]
+                for h in range(HALVES):
+                    nc.vector.tensor_tensor(
+                        mixed[:, pieces[h]], mixed[:, pieces[h]], weighted[k - 1][:, pieces[h]], ADD
+                    )
 
         result = held.tile([G, N], F32, name="result")
-        nc.vector.tensor_scalar(result[:], mixed[:], bias[:, 0:1], 0.0, op0=ADD, op1=MAX)
-        nc.sync.dma_start(out, result[:])
+        queues = [nc.sync, nc.scalar]
+        for h in range(HALVES):
+            nc.vector.tensor_scalar(
+                result[:, pieces[h]], mixed[:, pieces[h]], bias[:, 0:1], 0.0, op0=ADD, op1=MAX
+            )
+            queues[h].dma_start(out[:, pieces[h]], result[:, pieces[h]])

@@ -57,19 +57,18 @@ def tile_sgcn_kernel(tc, table, w, ew, b, offs, out):
         weighted = [held.tile([G, N], F32, name=f"weighted{k}") for k in range(K)]
         mixed = weighted[0]
         pieces = [slice(h * H, (h + 1) * H) for h in range(HALVES)]
-        for k in range(K + 1):
-            if k < K:
+        for k in range(K):
+            for h in range(HALVES):
+                nc.vector.tensor_tensor(
+                    weighted[k][:, pieces[h]],
+                    projected[k][h][:],
+                    edge_weights[k][:, pieces[h]],
+                    MULT,
+                )
+            if k > 0:
                 for h in range(HALVES):
                     nc.vector.tensor_tensor(
-                        weighted[k][:, pieces[h]],
-                        projected[k][h][:],
-                        edge_weights[k][:, pieces[h]],
-                        MULT,
-                    )
-            if k >= 2:
-                for h in range(HALVES):
-                    nc.vector.tensor_tensor(
-                        mixed[:, pieces[h]], mixed[:, pieces[h]], weighted[k - 1][:, pieces[h]], ADD
+                        mixed[:, pieces[h]], mixed[:, pieces[h]], weighted[k][:, pieces[h]], ADD
                     )
 
         result = held.tile([G, N], F32, name="result")

@@ -34,7 +34,13 @@ def tile_sgcn_kernel(tc, table, w, ew, b, offs, out):
         edge_weights = []
         for k in range(K):
             row = held.tile([G, N], F32, name=f"edge_weights{k}")
-            nc.scalar.dma_start(row[:], ew[k, :].partition_broadcast(G))
+            if k < K - 1:
+                nc.scalar.dma_start(row[:], ew[k, :].partition_broadcast(G))
+            else:
+                for h in range(HALVES):
+                    nc.scalar.dma_start(
+                        row[:, h * H : (h + 1) * H], ew[k, h * H : (h + 1) * H].partition_broadcast(G)
+                    )
             edge_weights.append(row)
         bias = held.tile([G, 1], F32, name="bias")
         nc.sync.dma_start(bias[:], b)

@@ -72,8 +72,9 @@ def tile_sgcn_kernel(tc, table, w, ew, b, offs, out):
                     MULT,
                 )
             if k > 0:
+                adder = nc.gpsimd if k == 1 else nc.vector
                 for h in range(HALVES):
-                    nc.vector.tensor_tensor(
+                    adder.tensor_tensor(
                         mixed[:, pieces[h]], mixed[:, pieces[h]], weighted[k][:, pieces[h]], ADD
                     )
 

@@ -5,6 +5,7 @@ S = 1024
 N = 512
 K = 4
 G = 128
+B = G // K
 HALVES = 2
 H = N // HALVES
 
@@ -31,57 +32,65 @@ def tile_sgcn_kernel(tc, table, w, ew, b, offs, out):
         kernels = held.tile([C, K * G], BF16, name="kernels")
         nc.scalar.dma_start(kernels[:], w)
 
-        edge_weights = []
+        edge_weights = held.tile([K * B, N], F32, name="edge_weights")
         for k in range(K):
-            row = held.tile([G, N], F32, name=f"edge_weights{k}")
-            if k < K - 1:
-                nc.scalar.dma_start(row[:], ew[k, :].partition_broadcast(G))
-            else:
-                for h in range(HALVES):
-                    nc.scalar.dma_start(
-                        row[:, h * H : (h + 1) * H], ew[k, h * H : (h + 1) * H].partition_broadcast(G)
-                    )
-            edge_weights.append(row)
+            nc.scalar.dma_start(
+                edge_weights[k * B : (k + 1) * B, :], ew[k, :].partition_broadcast(B)
+            )
         bias = held.tile([G, 1], F32, name="bias")
         nc.sync.dma_start(bias[:], b)
 
-        projected = [
-            [psum.tile([G, H], F32, name=f"projected{k}_{h}") for h in range(HALVES)]
-            for k in range(K)
-        ]
-
+        fold = held.tile([K * B, B], F32, name="fold")
+        nc.gpsimd.memset(fold[:], 0.0)
         for k in range(K):
-            for h in range(HALVES):
+            nc.gpsimd.affine_select(
+                out=fold[:],
+                in_=fold[:],
+                compare_op=mybir.AluOpType.not_equal,
+                fill=1.0,
+                base=-k * B,
+                pattern=[[-1, B]],
+                channel_multiplier=1,
+            )
+
+        kernel_columns = kernels[:].rearrange("c (k m i) -> c k m i", k=K, m=G // B)
+        blocks = []
+        for m in range(G // B):
+            block = held.tile([C, K * B], BF16, name=f"block{m}")
+            nc.vector.tensor_copy(
+                block[:].rearrange("c (k i) -> c k i", k=K), kernel_columns[:, :, m, :]
+            )
+            blocks.append(block)
+
+        weighted = [held.tile([K * B, N], F32, name=f"weighted{m}") for m in range(G // B)]
+        pieces = [slice(h * H, (h + 1) * H) for h in range(HALVES)]
+        for h in range(HALVES):
+            for m in range(G // B):
+                projected = psum.tile([K * B, H], F32, name="projected", bufs=6)
                 nc.tensor.matmul(
-                    projected[k][h][:],
-                    kernels[:, k * G : (k + 1) * G],
+                    projected[:],
+                    blocks[m][:],
                     nodes[:].indirect(offsets[:, h * (H // 16) : (h + 1) * (H // 16)]),
                     start=True,
                     stop=True,
                 )
-
-        weighted = [held.tile([G, N], F32, name=f"weighted{k}") for k in range(K)]
-        mixed = weighted[0]
-        pieces = [slice(h * H, (h + 1) * H) for h in range(HALVES)]
-        for k in range(K):
-            for h in range(HALVES):
                 nc.vector.tensor_tensor(
-                    weighted[k][:, pieces[h]],
-                    projected[k][h][:],
-                    edge_weights[k][:, pieces[h]],
-                    MULT,
+                    weighted[m][:, pieces[h]], projected[:], edge_weights[:, pieces[h]], MULT
                 )
-            if k > 0:
-                adder = nc.gpsimd if k == 1 else nc.vector
-                for h in range(HALVES):
-                    adder.tensor_tensor(
-                        mixed[:, pieces[h]], mixed[:, pieces[h]], weighted[k][:, pieces[h]], ADD
-                    )
 
         result = held.tile([G, N], F32, name="result")
         queues = [nc.sync, nc.scalar]
         for h in range(HALVES):
+            mixed = psum.tile([G, H], F32, name="mixed", bufs=2)
+            for m in range(G // B):
+                nc.tensor.matmul(
+                    mixed[m * B : (m + 1) * B, :],
+                    fold[:],
+                    weighted[m][:, pieces[h]],
+                    start=True,
+                    stop=True,
+                )
             nc.vector.tensor_scalar(
-                result[:, pieces[h]], mixed[:, pieces[h]], bias[:, 0:1], 0.0, op0=ADD, op1=MAX
+                result[:, pieces[h]], mixed[:], bias[:, 0:1], 0.0, op0=ADD, op1=MAX
             )
             queues[h].dma_start(out[:, pieces[h]], result[:, pieces[h]])

@@ -34,11 +34,11 @@ def tile_sgcn_kernel(tc, table, w, ew, b, offs, out):
 
         edge_weights = held.tile([K * B, N], F32, name="edge_weights")
         for k in range(K):
-            nc.scalar.dma_start(
+            nc.sync.dma_start(
                 edge_weights[k * B : (k + 1) * B, :], ew[k, :].partition_broadcast(B)
             )
         bias = held.tile([G, 1], F32, name="bias")
-        nc.sync.dma_start(bias[:], b)
+        nc.scalar.dma_start(bias[:], b)
 
         fold = held.tile([K * B, B], F32, name="fold")
         nc.gpsimd.memset(fold[:], 0.0)

@@ -27,16 +27,15 @@ def tile_sgcn_kernel(tc, table, w, ew, b, offs, out):
     ):
         offsets = held.tile([128, N // 16], U16, name="offsets")
         nc.sync.dma_start(offsets[:], offs)
+
+        ew_rows = held.tile([K * B, B], F32, name="ew_rows", align_bytes=64)
+        ew_in_rows = ew.rearrange("k (b e) -> (k b) e", e=B)
+        nc.sync.dma_start(ew_rows[0::2, :], ew_in_rows)
         nodes = held.tile([C, S], BF16, name="nodes")
         nc.sync.dma_start(nodes[:], table)
         kernels = held.tile([C, K * G], BF16, name="kernels")
         nc.scalar.dma_start(kernels[:], w)
-
-        edge_weights = held.tile([K * B, N], F32, name="edge_weights")
-        for k in range(K):
-            nc.sync.dma_start(
-                edge_weights[k * B : (k + 1) * B, :], ew[k, :].partition_broadcast(B)
-            )
+        nc.scalar.dma_start(ew_rows[1::2, :], ew_in_rows)
         bias = held.tile([G, 1], F32, name="bias")
         nc.scalar.dma_start(bias[:], b)
 
@@ -61,6 +60,16 @@ def tile_sgcn_kernel(tc, table, w, ew, b, offs, out):
                 block[:].rearrange("c (k i) -> c k i", k=K), kernel_columns[:, :, m, :]
             )
             blocks.append(block)
+
+        ew_columns = held.tile([K * B, B], F32, name="ew_columns", align_bytes=64)
+        nc.vector.transpose(ew_columns[:], ew_rows[:])
+        ew_repeated = held.tile([K * B, N], F32, name="ew_repeated", align_bytes=64)
+        nc.vector.tensor_copy(
+            ew_repeated[:].rearrange("p (b i) -> p b i", i=B),
+            ew_columns[:, 0::2].unsqueeze(2).to_broadcast([K * B, N // B, B]),
+        )
+        edge_weights = held.tile([K * B, N], F32, name="edge_weights", align_bytes=64)
+        nc.vector.transpose(edge_weights[:], ew_repeated[:])
 
         weighted = [held.tile([K * B, N], F32, name=f"weighted{m}") for m in range(G // B)]
         pieces = [slice(h * H, (h + 1) * H) for h in range(HALVES)]

import concourse.mybir as mybir

C = 128
S = 1024
N = 512
K = 4
G = 128
B = G // K
HALVES = 2
H = N // HALVES

FLOPS = 2 * C * K * G * N

BF16 = mybir.dt.bfloat16
F32 = mybir.dt.float32
U16 = mybir.dt.uint16
MULT = mybir.AluOpType.mult
ADD = mybir.AluOpType.add
MAX = mybir.AluOpType.max


def tile_sgcn_kernel(tc, table, w, ew, b, offs, out):
    nc = tc.nc
    with (
        tc.tile_pool(name="held", bufs=1) as held,
        tc.psum_pool(name="psum", bufs=1) as psum,
    ):
        offsets = held.tile([128, N // 16], U16, name="offsets")
        nc.sync.dma_start(offsets[:], offs)

        ew_rows = held.tile([K * B, B], F32, name="ew_rows", align_bytes=64)
        ew_in_rows = ew.rearrange("k (b e) -> (k b) e", e=B)
        nc.sync.dma_start(ew_rows[0::2, :], ew_in_rows)
        nodes = held.tile([C, S], BF16, name="nodes")
        nc.sync.dma_start(nodes[:], table)
        kernels = held.tile([C, K * G], BF16, name="kernels")
        nc.scalar.dma_start(kernels[:], w)
        nc.scalar.dma_start(ew_rows[1::2, :], ew_in_rows)
        bias = held.tile([G, 1], F32, name="bias")
        nc.scalar.dma_start(bias[:], b)

        fold = held.tile([K * B, B], F32, name="fold")
        nc.gpsimd.memset(fold[:], 0.0)
        for k in range(K):
            nc.gpsimd.affine_select(
                out=fold[:],
                in_=fold[:],
                compare_op=mybir.AluOpType.not_equal,
                fill=1.0,
                base=-k * B,
                pattern=[[-1, B]],
                channel_multiplier=1,
            )

        kernel_columns = kernels[:].rearrange("c (k m i) -> c k m i", k=K, m=G // B)
        blocks = []
        for m in range(G // B):
            block = held.tile([C, K * B], BF16, name=f"block{m}")
            nc.vector.tensor_copy(
                block[:].rearrange("c (k i) -> c k i", k=K), kernel_columns[:, :, m, :]
            )
            blocks.append(block)

        ew_columns = held.tile([K * B, B], F32, name="ew_columns", align_bytes=64)
        nc.vector.transpose(ew_columns[:], ew_rows[:])
        ew_repeated = held.tile([K * B, N], F32, name="ew_repeated", align_bytes=64)
        nc.vector.tensor_copy(
            ew_repeated[:].rearrange("p (b i) -> p b i", i=B),
            ew_columns[:, 0::2].unsqueeze(2).to_broadcast([K * B, N // B, B]),
        )
        edge_weights = held.tile([K * B, N], F32, name="edge_weights", align_bytes=64)
        nc.vector.transpose(edge_weights[:], ew_repeated[:])

        weighted = [held.tile([K * B, N], F32, name=f"weighted{m}") for m in range(G // B)]
        pieces = [slice(h * H, (h + 1) * H) for h in range(HALVES)]
        for h in range(HALVES):
            for m in range(G // B):
                projected = psum.tile([K * B, H], F32, name="projected", bufs=6)
                nc.tensor.matmul(
                    projected[:],
                    blocks[m][:],
                    nodes[:].indirect(offsets[:, h * (H // 16) : (h + 1) * (H // 16)]),
                    start=True,
                    stop=True,
                )
                nc.vector.tensor_tensor(
                    weighted[m][:, pieces[h]], projected[:], edge_weights[:, pieces[h]], MULT
                )

        result = held.tile([G, N], F32, name="result")
        queues = [nc.sync, nc.scalar]
        for h in range(HALVES):
            mixed = psum.tile([G, H], F32, name="mixed", bufs=2)
            for m in range(G // B):
                nc.tensor.matmul(
                    mixed[m * B : (m + 1) * B, :],
                    fold[:],
                    weighted[m][:, pieces[h]],
                    start=True,
                    stop=True,
                )
            nc.vector.tensor_scalar(
                result[:, pieces[h]], mixed[:], bias[:, 0:1], 0.0, op0=ADD, op1=MAX
            )
            queues[h].dma_start(out[:, pieces[h]], result[:, pieces[h]])
